import numpy as np
import ml_dtypes


def mxq(x, axis, fmt="e4m3"):
    dtype, down = {"e4m3": (ml_dtypes.float8_e4m3fn, 7), "e5m2": (ml_dtypes.float8_e5m2, 14)}[fmt]
    v = np.moveaxis(np.asarray(x, np.float32).astype(ml_dtypes.bfloat16).astype(np.float64), axis, -1)
    blocks = v.reshape(v.shape[:-1] + (-1, 32))
    amax = np.abs(blocks).max(-1, keepdims=True)
    byte = np.maximum(np.where(amax > 0, np.frexp(amax)[1] - 1 + 127, 0) - down, 1)
    scale = np.exp2(byte - 127.0)
    codes = (blocks / scale).astype(np.float32).astype(dtype).astype(np.float64)
    return np.moveaxis((codes * scale).reshape(v.shape), -1, axis)


WIDE = False


def mx_kscale(k):
    if not WIDE:
        return np.ones(k)
    levels = np.array([10, -10, 5, -5, 0])
    a = np.random.permutation(np.resize(levels, k // 512 * 4)).reshape(k // 512, 4)
    idx = np.arange(k)
    return np.exp2(a[idx // 512, idx % 128 // 32])


BF16 = ml_dtypes.bfloat16


def bf(x):
    return np.asarray(x, np.float32).astype(BF16)


def f64(x):
    return np.asarray(x).astype(np.float64)


B, LA, LB, D = 2, 4096, 512, 512


def setup_inputs():
    s = mx_kscale(D)
    return {"a": bf(np.random.standard_normal((B, LA, D)) * 1.5 * s), "b": bf(np.random.standard_normal((B, LB, D)) * 1.5 / s)}


def reference(a, b):
    a, b = f64(a), f64(b)
    scale = 1.0 / np.sqrt(D)
    simi = (mxq(a, 2, "e4m3") @ mxq(b, 2, "e4m3").transpose(0, 2, 1)) * scale
    e = np.exp(simi - simi.max(2, keepdims=True))
    return (mxq(e, 2, "e4m3") @ mxq(b, 1, "e4m3")) / e.sum(2, keepdims=True) + a

@@ -1,0 +1,255 @@
+import math
+from contextlib import ExitStack
+
+import concourse.mybir as mybir
+from concourse.masks import make_identity
+
+F32 = mybir.dt.float32
+BF16 = mybir.dt.bfloat16
+U32 = mybir.dt.uint32
+U8 = mybir.dt.uint8
+FP8X4 = mybir.dt.float8_e4m3fn_x4
+ALU = mybir.AluOpType
+ACT = mybir.ActivationFunctionType
+AX = mybir.AxisListType
+
+P = 128
+NBATCH, LA, LB, D = 2, 4096, 512, 512
+SCALE = 1.0 / math.sqrt(D)
+NPAIR = NBATCH * LA // (2 * P)
+PAIRS_PER_BATCH = NPAIR // NBATCH
+NGROUP = NPAIR // 2
+
+FLOPS = 2 * 2 * NBATCH * LA * LB * D
+
+
+def tile_intra_t_kernel(tc, a, b, out):
+    nc = tc.nc
+    a_v = a.rearrange("n (g p t) d -> (n g) p (t d)", p=P, t=4)
+    o_v = out.rearrange("n (g p t) d -> (n g) p (t d)", p=P, t=4)
+    b_v = b.rearrange("n (c t) d -> n c (t d)", t=4)
+
+    with ExitStack() as ctx:
+        keep = ctx.enter_context(tc.tile_pool(name="keep", bufs=1))
+        w3 = ctx.enter_context(tc.tile_pool(name="w3", bufs=3))
+        w4 = ctx.enter_context(tc.tile_pool(name="w4", bufs=4))
+        w6 = ctx.enter_context(tc.tile_pool(name="w6", bufs=6))
+        psum = ctx.enter_context(tc.psum_pool(name="psum", bufs=1))
+        ctx.enter_context(tc.manual_schedule())
+
+        def bank(k, shape, dtype, name):
+            return psum.tile(shape, dtype, tag="bank%d" % k, name=name)
+
+        b_sb = [keep.tile([P, 4 * D], BF16, name="b_sb%d" % n) for n in range(NBATCH)]
+        a_sb = [keep.tile([P, 4 * D], BF16, name="a_sb%d" % g) for g in range(NGROUP)]
+        nc.sync.dma_start(out=b_sb[0][:], in_=b_v[0, :, :])
+        nc.sync.dma_start(out=a_sb[0][:], in_=a_v[0, :, :])
+        nc.sync.dma_start(out=b_sb[1][:], in_=b_v[1, :, :])
+        for g in range(1, NGROUP):
+            nc.sync.dma_start(out=a_sb[g][:], in_=a_v[g, :, :])
+
+        ident_f = keep.tile([P, P], F32, name="ident_f")
+        make_identity(nc, ident_f[:])
+        ident_b = keep.tile([P, P], BF16, name="ident_b")
+        make_identity(nc, ident_b[:])
+        warm = keep.tile([P, 1], F32, name="warm")
+        warm2 = keep.tile([P, 1], F32, name="warm2")
+        nc.vector.memset(warm[:], 0.0)
+        nc.scalar.activation(out=warm2[:], in_=warm[:], func=ACT.Exp)
+
+        bt_c = [keep.tile([P, LB], U32, name="bt_c%d" % n, align_bytes=64) for n in range(NBATCH)]
+        bt_s = [keep.tile([P, LB], U8, name="bt_s%d" % n, align_bytes=64) for n in range(NBATCH)]
+        b2_c = [keep.tile([P, D], U32, name="b2_c%d" % n, align_bytes=64) for n in range(NBATCH)]
+        b2_s = [keep.tile([P, D], U8, name="b2_s%d" % n, align_bytes=64) for n in range(NBATCH)]
+        gb = [keep.tile([P, 4 * D], BF16, name="gb%d" % n, align_bytes=64) for n in range(NBATCH)]
+
+        st = {}
+
+        def unit_src(unit, s):
+            kind, x, h = unit
+            src = a_sb[x] if kind == "a" else b_sb[x]
+            t = 2 * h + s
+            return src[:].bitcast(F32)[:, t * 256:(t + 1) * 256]
+
+        def a_unit(j):
+            return ("a", j // 2, j % 2)
+
+        def ta(unit, k):
+            at = bank(k, [P, 2, 2, P], F32, "at")
+            st[("at", unit)] = at
+            for s in range(2):
+                src = unit_src(unit, s)
+                for u in range(2):
+                    nc.tensor.transpose(at[:, s, u, :], src[:, u * P:(u + 1) * P], ident_f[:])
+
+        def xa(unit, eng):
+            at = st[("at", unit)]
+            ga = w4.tile([P, 8 * P], BF16, name="ga", tag="ga", align_bytes=64)
+            st[("ga", unit)] = ga
+            o = ga[:].bitcast(F32).rearrange("p (s r u) -> p s r u", s=2, u=2)
+            i = at[:].rearrange("p s u r -> p s r u")
+            if eng == "S":
+                nc.scalar.copy(out=o, in_=i)
+            else:
+                nc.vector.tensor_copy(out=o, in_=i)
+
+        def qa(unit):
+            kind, x, h = unit
+            ga = st[("ga", unit)]
+            if kind == "a":
+                ac = w4.tile([P, 2 * P], U32, name="ac", tag="ac", align_bytes=64)
+                asc = w4.tile([P, 2 * P], U8, name="asc", tag="asc", align_bytes=64)
+                st[("ac", unit)] = (ac, asc)
+                codes, plane = ac[:], asc[:]
+            else:
+                codes = bt_c[x][:, h * 256:(h + 1) * 256]
+                plane = bt_s[x][:, h * 256:(h + 1) * 256]
+            nc.vector.quantize_mx(out=codes.bitcast(FP8X4), scales=plane, in_=ga[:])
+
+        def rg(n):
+            nc.vector.tensor_copy(
+                out=gb[n][:].rearrange("p (c i t) -> p c t i", i=4, t=4),
+                in_=b_sb[n][:].rearrange("p (t c i) -> p c t i", t=4, i=4),
+            )
+
+        def qb2(n):
+            nc.vector.quantize_mx(out=b2_c[n][:].bitcast(FP8X4), scales=b2_s[n][:], in_=gb[n][:])
+
+        def m1(j):
+            n = j // PAIRS_PER_BATCH
+            ac, asc = st[("ac", a_unit(j))]
+            for s in range(2):
+                sc = bank((j % 2) * 2 + s, [P, LB], F32, "sc")
+                st[("sc", j, s)] = sc
+                nc.tensor.matmul_mx(
+                    out=sc[:],
+                    lhsT=ac[:, s * P:(s + 1) * P].bitcast(FP8X4),
+                    lhsT_scale=asc[:, s * P:(s + 1) * P],
+                    rhs=bt_c[n][:].bitcast(FP8X4),
+                    rhs_scale=bt_s[n][:],
+                    start=True,
+                    stop=True,
+                )
+
+        def mx_(j):
+            mx = w6.tile([P, 2], F32, name="mx", tag="mx")
+            nb = w6.tile([P, 2], F32, name="nb", tag="nb")
+            st[("nb", j)] = nb
+            for s in range(2):
+                nc.vector.reduce_max(out=mx[:, s:s + 1], in_=st[("sc", j, s)][:], axis=AX.X)
+            nc.gpsimd.tensor_scalar(out=nb[:], in0=mx[:], scalar1=-SCALE, scalar2=0.0,
+                                    op0=ALU.mult, op1=ALU.add)
+
+        def ex(j):
+            e = w3.tile([P, 2, LB], BF16, name="e", tag="e")
+            rs = w6.tile([P, 2], F32, name="rs", tag="rs")
+            st[("e", j)] = e
+            st[("rs", j)] = rs
+            nb = st[("nb", j)]
+            for s in range(2):
+                nc.scalar.activation(out=e[:, s, :], in_=st[("sc", j, s)][:], func=ACT.Exp,
+                                     bias=nb[:, s:s + 1], scale=SCALE, accum_out=rs[:, s:s + 1])
+
+        def te(j):
+            e = st[("e", j)]
+            et = bank(7, [P, 2, 4, P], BF16, "et")
+            st[("et", j)] = et
+            for s in range(2):
+                for t in range(4):
+                    nc.tensor.transpose(et[:, s, t, :], e[:, s, t * P:(t + 1) * P], ident_b[:])
+
+        def xe(j):
+            et = st[("et", j)]
+            ge = w3.tile([P, 8 * P], BF16, name="ge", tag="ge", align_bytes=64)
+            st[("ge", j)] = ge
+            nc.scalar.copy(out=ge[:].rearrange("p (s r t) -> p s r t", s=2, t=4),
+                           in_=et[:].rearrange("p s t r -> p s r t"))
+
+        def qe(j):
+            ec = w3.tile([P, 2 * P], U32, name="ec", tag="ec", align_bytes=64)
+            es = w3.tile([P, 2 * P], U8, name="es", tag="es", align_bytes=64)
+            st[("ec", j)] = (ec, es)
+            nc.vector.quantize_mx(out=ec[:].bitcast(FP8X4), scales=es[:], in_=st[("ge", j)][:])
+
+        def m2(j):
+            n = j // PAIRS_PER_BATCH
+            ec, es = st[("ec", j)]
+            for s in range(2):
+                oc = bank(4 + s, [P, D], F32, "oc")
+                st[("oc", j, s)] = oc
+                nc.tensor.matmul_mx(
+                    out=oc[:],
+                    lhsT=ec[:, s * P:(s + 1) * P].bitcast(FP8X4),
+                    lhsT_scale=es[:, s * P:(s + 1) * P],
+                    rhs=b2_c[n][:].bitcast(FP8X4),
+                    rhs_scale=b2_s[n][:],
+                    start=True,
+                    stop=True,
+                )
+
+        def fin(j):
+            g, h = j // 2, j % 2
+            ri = w6.tile([P, 2], F32, name="ri", tag="ri")
+            ob = w4.tile([P, 2, D], F32, name="ob", tag="ob")
+            nc.vector.reciprocal(out=ri[:], in_=st[("rs", j)][:])
+            for s in range(2):
+                t = 2 * h + s
+                nc.vector.scalar_tensor_tensor(
+                    out=ob[:, s, :], in0=st[("oc", j, s)][:], scalar=ri[:, s:s + 1],
+                    in1=a_sb[g][:, t * D:(t + 1) * D], op0=ALU.mult, op1=ALU.add)
+            nc.sync.dma_start(out=o_v[g, :, h * 2 * D:(h + 1) * 2 * D],
+                              in_=ob[:].rearrange("p s d -> p (s d)"))
+
+        ub = [[("b", n, h) for h in range(2)] for n in range(NBATCH)]
+        ta(ub[0][0], 6)
+        ta(ub[0][1], 7)
+        xa(ub[0][0], "S")
+        xa(ub[0][1], "V")
+        ta(a_unit(0), 4)
+        ta(a_unit(1), 5)
+        qa(ub[0][0])
+        qa(ub[0][1])
+        xa(a_unit(0), "S")
+        xa(a_unit(1), "S")
+        qa(a_unit(0))
+        qa(a_unit(1))
+
+        def live(j):
+            return 0 <= j < NPAIR
+
+        for i in range(-2, NPAIR + 2):
+            if live(i - 1):
+                qe(i - 1)
+                m2(i - 1)
+            if live(i + 1):
+                mx_(i + 1)
+            if live(i):
+                ex(i)
+                te(i)
+            if 2 <= i + 3 < NPAIR:
+                xa(a_unit(i + 3), "S")
+            if i == -1:
+                xa(ub[1][0], "S")
+                xa(ub[1][1], "S")
+            if 2 <= i + 2 < NPAIR:
+                qa(a_unit(i + 2))
+            if live(i):
+                xe(i)
+            if 2 <= i + 4 < NPAIR:
+                ta(a_unit(i + 4), 6)
+            if live(i + 2):
+                m1(i + 2)
+            if i == -2:
+                ta(ub[1][0], 4)
+                ta(ub[1][1], 5)
+            if i == -1:
+                rg(0)
+            if i == 0:
+                qb2(0)
+                qa(ub[1][0])
+                qa(ub[1][1])
+                rg(1)
+            if i == 1:
+                qb2(1)
+            if live(i - 1):
+                fin(i - 1)

@@ -54,7 +54,9 @@ def tile_intra_t_kernel(tc, a, b, out):
         make_identity(nc, ident_b[:])
         warm = keep.tile([P, 1], F32, name="warm")
         warm2 = keep.tile([P, 1], F32, name="warm2")
+        neg1 = keep.tile([P, 2], F32, name="neg1")
         nc.vector.memset(warm[:], 0.0)
+        nc.vector.memset(neg1[:], -1.0)
         nc.scalar.activation(out=warm2[:], in_=warm[:], func=ACT.Exp)
 
         bt_c = [keep.tile([P, LB], U32, name="bt_c%d" % n, align_bytes=64) for n in range(NBATCH)]
@@ -86,12 +88,12 @@ def tile_intra_t_kernel(tc, a, b, out):
             at = st[("at", unit)]
             ga = w4.tile([P, 8 * P], BF16, name="ga", tag="ga", align_bytes=64)
             st[("ga", unit)] = ga
-            o = ga[:].bitcast(F32).rearrange("p (s r u) -> p s r u", s=2, u=2)
-            i = at[:].rearrange("p s u r -> p s r u")
+            dst = ga[:].bitcast(F32).rearrange("p (s r u) -> p s r u", s=2, u=2)
+            src = at[:].rearrange("p s u r -> p s r u")
             if eng == "S":
-                nc.scalar.copy(out=o, in_=i)
+                nc.scalar.copy(out=dst, in_=src)
             else:
-                nc.vector.tensor_copy(out=o, in_=i)
+                nc.vector.tensor_copy(out=dst, in_=src)
 
         def qa(unit):
             kind, x, h = unit
@@ -106,53 +108,63 @@ def tile_intra_t_kernel(tc, a, b, out):
                 plane = bt_s[x][:, h * 256:(h + 1) * 256]
             nc.vector.quantize_mx(out=codes.bitcast(FP8X4), scales=plane, in_=ga[:])
 
-        def rg(n):
-            nc.vector.tensor_copy(
-                out=gb[n][:].rearrange("p (c i t) -> p c t i", i=4, t=4),
-                in_=b_sb[n][:].rearrange("p (t c i) -> p c t i", t=4, i=4),
-            )
+        def rg(n, piece, pieces, eng):
+            w = D // pieces
+            dst = gb[n][:, piece * 4 * w:(piece + 1) * 4 * w].rearrange("p (c i t) -> p c t i", i=4, t=4)
+            src = b_sb[n][:].rearrange("p (t d) -> p t d", t=4)[:, :, piece * w:(piece + 1) * w]
+            src = src.rearrange("p t (c i) -> p c t i", i=4)
+            if eng == "V":
+                nc.vector.tensor_copy(out=dst, in_=src)
+            else:
+                nc.gpsimd.tensor_scalar(out=dst, in0=src, scalar1=1.0, scalar2=0.0,
+                                        op0=ALU.mult, op1=ALU.add)
 
         def qb2(n):
             nc.vector.quantize_mx(out=b2_c[n][:].bitcast(FP8X4), scales=b2_s[n][:], in_=gb[n][:])
 
-        def m1(j):
+        def m1(j, s):
             n = j // PAIRS_PER_BATCH
             ac, asc = st[("ac", a_unit(j))]
-            for s in range(2):
-                sc = bank((j % 2) * 2 + s, [P, LB], F32, "sc")
-                st[("sc", j, s)] = sc
-                nc.tensor.matmul_mx(
-                    out=sc[:],
-                    lhsT=ac[:, s * P:(s + 1) * P].bitcast(FP8X4),
-                    lhsT_scale=asc[:, s * P:(s + 1) * P],
-                    rhs=bt_c[n][:].bitcast(FP8X4),
-                    rhs_scale=bt_s[n][:],
-                    start=True,
-                    stop=True,
-                )
+            sc = bank((2 * j + s) % 3, [P, LB], F32, "sc")
+            st[("sc", j, s)] = sc
+            nc.tensor.matmul_mx(
+                out=sc[:],
+                lhsT=ac[:, s * P:(s + 1) * P].bitcast(FP8X4),
+                lhsT_scale=asc[:, s * P:(s + 1) * P],
+                rhs=bt_c[n][:].bitcast(FP8X4),
+                rhs_scale=bt_s[n][:],
+                start=True,
+                stop=True,
+            )
 
-        def mx_(j):
-            mx = w6.tile([P, 2], F32, name="mx", tag="mx")
-            nb = w6.tile([P, 2], F32, name="nb", tag="nb")
-            st[("nb", j)] = nb
-            for s in range(2):
-                nc.vector.reduce_max(out=mx[:, s:s + 1], in_=st[("sc", j, s)][:], axis=AX.X)
-            nc.gpsimd.tensor_scalar(out=nb[:], in0=mx[:], scalar1=-SCALE, scalar2=0.0,
+        def mx_(j, s):
+            if s == 0:
+                st[("mx", j)] = w6.tile([P, 2], F32, name="mx", tag="mx")
+                st[("nb", j)] = w6.tile([P, 2], F32, name="nb", tag="nb")
+            mx = st[("mx", j)]
+            nb = st[("nb", j)]
+            nc.vector.reduce_max(out=mx[:, s:s + 1], in_=st[("sc", j, s)][:], axis=AX.X)
+            nc.gpsimd.tensor_scalar(out=nb[:, s:s + 1], in0=mx[:, s:s + 1], scalar1=-SCALE, scalar2=0.0,
                                     op0=ALU.mult, op1=ALU.add)
 
-        def ex(j):
-            e = w3.tile([P, 2, LB], BF16, name="e", tag="e")
-            rs = w6.tile([P, 2], F32, name="rs", tag="rs")
-            st[("e", j)] = e
-            st[("rs", j)] = rs
+        def ex(j, s):
+            if s == 0:
+                st[("e", j)] = w3.tile([P, 2, LB], BF16, name="e", tag="e")
+                st[("rs", j)] = w6.tile([P, 2], F32, name="rs", tag="rs")
+            e = st[("e", j)]
+            rs = st[("rs", j)]
             nb = st[("nb", j)]
-            for s in range(2):
-                nc.scalar.activation(out=e[:, s, :], in_=st[("sc", j, s)][:], func=ACT.Exp,
-                                     bias=nb[:, s:s + 1], scale=SCALE, accum_out=rs[:, s:s + 1])
+            nc.scalar.activation(out=e[:, s, :], in_=st[("sc", j, s)][:], func=ACT.Exp,
+                                 bias=nb[:, s:s + 1], scale=SCALE, accum_out=rs[:, s:s + 1])
+
+        def rc(j):
+            ri = w6.tile([P, 2], F32, name="ri", tag="ri")
+            st[("ri", j)] = ri
+            nc.gpsimd.tensor_tensor(out=ri[:], in0=st[("rs", j)][:], in1=neg1[:], op=ALU.pow)
 
         def te(j):
             e = st[("e", j)]
-            et = bank(7, [P, 2, 4, P], BF16, "et")
+            et = bank(6 + j % 2, [P, 2, 4, P], BF16, "et")
             st[("et", j)] = et
             for s in range(2):
                 for t in range(4):
@@ -171,85 +183,107 @@ def tile_intra_t_kernel(tc, a, b, out):
             st[("ec", j)] = (ec, es)
             nc.vector.quantize_mx(out=ec[:].bitcast(FP8X4), scales=es[:], in_=st[("ge", j)][:])
 
-        def m2(j):
+        def m2(j, s):
             n = j // PAIRS_PER_BATCH
             ec, es = st[("ec", j)]
-            for s in range(2):
-                oc = bank(4 + s, [P, D], F32, "oc")
-                st[("oc", j, s)] = oc
-                nc.tensor.matmul_mx(
-                    out=oc[:],
-                    lhsT=ec[:, s * P:(s + 1) * P].bitcast(FP8X4),
-                    lhsT_scale=es[:, s * P:(s + 1) * P],
-                    rhs=b2_c[n][:].bitcast(FP8X4),
-                    rhs_scale=b2_s[n][:],
-                    start=True,
-                    stop=True,
-                )
+            oc = bank(3 + s, [P, D], F32, "oc")
+            st[("oc", j, s)] = oc
+            nc.tensor.matmul_mx(
+                out=oc[:],
+                lhsT=ec[:, s * P:(s + 1) * P].bitcast(FP8X4),
+                lhsT_scale=es[:, s * P:(s + 1) * P],
+                rhs=b2_c[n][:].bitcast(FP8X4),
+                rhs_scale=b2_s[n][:],
+                start=True,
+                stop=True,
+            )
 
-        def fin(j):
+        def fin(j, s):
             g, h = j // 2, j % 2
-            ri = w6.tile([P, 2], F32, name="ri", tag="ri")
-            ob = w4.tile([P, 2, D], F32, name="ob", tag="ob")
-            nc.vector.reciprocal(out=ri[:], in_=st[("rs", j)][:])
-            for s in range(2):
-                t = 2 * h + s
-                nc.vector.scalar_tensor_tensor(
-                    out=ob[:, s, :], in0=st[("oc", j, s)][:], scalar=ri[:, s:s + 1],
-                    in1=a_sb[g][:, t * D:(t + 1) * D], op0=ALU.mult, op1=ALU.add)
-            nc.sync.dma_start(out=o_v[g, :, h * 2 * D:(h + 1) * 2 * D],
-                              in_=ob[:].rearrange("p s d -> p (s d)"))
+            if s == 0:
+                st[("ob", j)] = w4.tile([P, 2, D], F32, name="ob", tag="ob")
+            ob = st[("ob", j)]
+            ri = st[("ri", j)]
+            t = 2 * h + s
+            nc.vector.scalar_tensor_tensor(
+                out=ob[:, s, :], in0=st[("oc", j, s)][:], scalar=ri[:, s:s + 1],
+                in1=a_sb[g][:, t * D:(t + 1) * D], op0=ALU.mult, op1=ALU.add)
+            if j == NPAIR - 1:
+                nc.sync.dma_start(out=o_v[g, :, t * D:(t + 1) * D], in_=ob[:, s, :])
+            elif s == 1:
+                nc.sync.dma_start(out=o_v[g, :, h * 2 * D:(h + 1) * 2 * D],
+                                  in_=ob[:].rearrange("p s d -> p (s d)"))
 
         ub = [[("b", n, h) for h in range(2)] for n in range(NBATCH)]
-        ta(ub[0][0], 6)
-        ta(ub[0][1], 7)
+        ta(ub[0][0], 5)
+        ta(ub[0][1], 6)
         xa(ub[0][0], "S")
         xa(ub[0][1], "V")
-        ta(a_unit(0), 4)
-        ta(a_unit(1), 5)
+        ta(a_unit(0), 7)
+        ta(a_unit(1), 3)
         qa(ub[0][0])
         qa(ub[0][1])
         xa(a_unit(0), "S")
         xa(a_unit(1), "S")
+        rg(0, 0, 2, "V")
         qa(a_unit(0))
         qa(a_unit(1))
+        rg(0, 1, 2, "V")
+        ta(ub[1][0], 4)
+        ta(ub[1][1], 2)
+        m1(0, 0)
+        m1(0, 1)
+        xa(ub[1][0], "S")
+        xa(ub[1][1], "S")
+        m1(1, 0)
+        ta(a_unit(2), 5)
+        mx_(0, 0)
+        mx_(0, 1)
+        qb2(0)
 
         def live(j):
             return 0 <= j < NPAIR
 
-        for i in range(-2, NPAIR + 2):
-            if live(i - 1):
-                qe(i - 1)
-                m2(i - 1)
+        for i in range(0, NPAIR + 4):
+            if live(i - 2):
+                qe(i - 2)
+                m2(i - 2, 0)
             if live(i + 1):
-                mx_(i + 1)
-            if live(i):
-                ex(i)
-                te(i)
-            if 2 <= i + 3 < NPAIR:
-                xa(a_unit(i + 3), "S")
-            if i == -1:
-                xa(ub[1][0], "S")
-                xa(ub[1][1], "S")
-            if 2 <= i + 2 < NPAIR:
-                qa(a_unit(i + 2))
-            if live(i):
-                xe(i)
-            if 2 <= i + 4 < NPAIR:
-                ta(a_unit(i + 4), 6)
-            if live(i + 2):
-                m1(i + 2)
-            if i == -2:
-                ta(ub[1][0], 4)
-                ta(ub[1][1], 5)
-            if i == -1:
-                rg(0)
+                mx_(i + 1, 0)
             if i == 0:
-                qb2(0)
                 qa(ub[1][0])
                 qa(ub[1][1])
-                rg(1)
-            if i == 1:
-                qb2(1)
+            if 1 <= i <= 4:
+                rg(1, i - 1, 4, "G")
+            if 3 <= i + 2 < NPAIR:
+                qa(a_unit(i + 2))
+            if live(i):
+                ex(i, 0)
+            if live(i + 1):
+                m1(i + 1, 1)
+            if live(i):
+                ex(i, 1)
+                rc(i)
+            if i == 0:
+                xa(a_unit(2), "S")
+                qa(a_unit(2))
+            if 3 <= i + 3 < NPAIR:
+                ta(a_unit(i + 3), 5)
+            if live(i):
+                te(i)
+            if live(i - 3):
+                fin(i - 3, 1)
+            if live(i - 2):
+                m2(i - 2, 1)
+            if live(i + 2):
+                m1(i + 2, 0)
             if live(i - 1):
-                fin(i - 1)
+                xe(i - 1)
+            if 3 <= i + 3 < NPAIR:
+                xa(a_unit(i + 3), "S")
+            if i == 6:
+                qb2(1)
+            if live(i + 1):
+                mx_(i + 1, 1)
+            if live(i - 2):
+                fin(i - 2, 0)

@@ -42,8 +42,10 @@ def tile_intra_t_kernel(tc, a, b, out):
 
         b_sb = [keep.tile([P, 4 * D], BF16, name="b_sb%d" % n) for n in range(NBATCH)]
         a_sb = [keep.tile([P, 4 * D], BF16, name="a_sb%d" % g) for g in range(NGROUP)]
-        nc.sync.dma_start(out=b_sb[0][:], in_=b_v[0, :, :])
-        nc.sync.dma_start(out=a_sb[0][:], in_=a_v[0, :, :])
+        for h in range(2):
+            nc.sync.dma_start(out=b_sb[0][:, h * 2 * D:(h + 1) * 2 * D], in_=b_v[0, :, h * 2 * D:(h + 1) * 2 * D])
+        for h in range(2):
+            nc.sync.dma_start(out=a_sb[0][:, h * 2 * D:(h + 1) * 2 * D], in_=a_v[0, :, h * 2 * D:(h + 1) * 2 * D])
         nc.sync.dma_start(out=b_sb[1][:], in_=b_v[1, :, :])
         for g in range(1, NGROUP):
             nc.sync.dma_start(out=a_sb[g][:], in_=a_v[g, :, :])
@@ -170,6 +172,28 @@ def tile_intra_t_kernel(tc, a, b, out):
                 for t in range(4):
                     nc.tensor.transpose(et[:, s, t, :], e[:, s, t * P:(t + 1) * P], ident_b[:])
 
+        def te1(j, s):
+            e = st[("e", j)]
+            et = bank(6 + s, [P, 4, P], BF16, "et1")
+            st[("et", j, s)] = et
+            for t in range(4):
+                nc.tensor.transpose(et[:, t, :], e[:, s, t * P:(t + 1) * P], ident_b[:])
+
+        def xe1(j, s):
+            ge = w3.tile([P, 4 * P], BF16, name="ge1", tag="ge1", align_bytes=64)
+            st[("ge", j, s)] = ge
+            nc.scalar.copy(out=ge[:].rearrange("p (r t) -> p r t", t=4),
+                           in_=st[("et", j, s)][:].rearrange("p t r -> p r t"))
+
+        def qe1(j, s):
+            if s == 0:
+                ec = w3.tile([P, 2 * P], U32, name="ec", tag="ec", align_bytes=64)
+                es = w3.tile([P, 2 * P], U8, name="es", tag="es", align_bytes=64)
+                st[("ec", j)] = (ec, es)
+            ec, es = st[("ec", j)]
+            nc.vector.quantize_mx(out=ec[:, s * P:(s + 1) * P].bitcast(FP8X4), scales=es[:, s * P:(s + 1) * P],
+                                  in_=st[("ge", j, s)][:])
+
         def xe(j):
             et = st[("et", j)]
             ge = w3.tile([P, 8 * P], BF16, name="ge", tag="ge", align_bytes=64)
@@ -183,10 +207,10 @@ def tile_intra_t_kernel(tc, a, b, out):
             st[("ec", j)] = (ec, es)
             nc.vector.quantize_mx(out=ec[:].bitcast(FP8X4), scales=es[:], in_=st[("ge", j)][:])
 
-        def m2(j, s):
+        def m2(j, s, k):
             n = j // PAIRS_PER_BATCH
             ec, es = st[("ec", j)]
-            oc = bank(3 + s, [P, D], F32, "oc")
+            oc = bank(k, [P, D], F32, "oc")
             st[("oc", j, s)] = oc
             nc.tensor.matmul_mx(
                 out=oc[:],
@@ -218,6 +242,7 @@ def tile_intra_t_kernel(tc, a, b, out):
         ta(ub[0][0], 5)
         ta(ub[0][1], 6)
         xa(ub[0][0], "S")
+        rg(0, 0, 2, "V")
         xa(ub[0][1], "V")
         ta(a_unit(0), 7)
         ta(a_unit(1), 3)
@@ -225,7 +250,6 @@ def tile_intra_t_kernel(tc, a, b, out):
         qa(ub[0][1])
         xa(a_unit(0), "S")
         xa(a_unit(1), "S")
-        rg(0, 0, 2, "V")
         qa(a_unit(0))
         qa(a_unit(1))
         rg(0, 1, 2, "V")
@@ -244,17 +268,19 @@ def tile_intra_t_kernel(tc, a, b, out):
         def live(j):
             return 0 <= j < NPAIR
 
-        for i in range(0, NPAIR + 4):
+        for i in range(0, NPAIR - 1):
+            if i == 3:
+                qb2(1)
             if live(i - 2):
                 qe(i - 2)
-                m2(i - 2, 0)
+                m2(i - 2, 0, 3)
             if live(i + 1):
                 mx_(i + 1, 0)
             if i == 0:
                 qa(ub[1][0])
                 qa(ub[1][1])
-            if 1 <= i <= 4:
-                rg(1, i - 1, 4, "G")
+            if i <= 1:
+                rg(1, 2 * i, 4, "G")
             if 3 <= i + 2 < NPAIR:
                 qa(a_unit(i + 2))
             if live(i):
@@ -274,16 +300,43 @@ def tile_intra_t_kernel(tc, a, b, out):
             if live(i - 3):
                 fin(i - 3, 1)
             if live(i - 2):
-                m2(i - 2, 1)
+                m2(i - 2, 1, 4)
             if live(i + 2):
                 m1(i + 2, 0)
             if live(i - 1):
                 xe(i - 1)
             if 3 <= i + 3 < NPAIR:
                 xa(a_unit(i + 3), "S")
-            if i == 6:
-                qb2(1)
             if live(i + 1):
                 mx_(i + 1, 1)
+            if i <= 1:
+                rg(1, 2 * i + 1, 4, "G")
             if live(i - 2):
                 fin(i - 2, 0)
+
+        z = NPAIR - 1
+        qe(z - 2)
+        m2(z - 2, 0, 3)
+        fin(z - 3, 1)
+        m2(z - 2, 1, 4)
+        xe(z - 1)
+        qe(z - 1)
+        ex(z, 0)
+        te1(z, 0)
+        m2(z - 1, 0, 1)
+        m2(z - 1, 1, 5)
+        ex(z, 1)
+        rc(z)
+        te1(z, 1)
+        fin(z - 2, 0)
+        fin(z - 2, 1)
+        fin(z - 1, 0)
+        xe1(z, 0)
+        qe1(z, 0)
+        m2(z, 0, 3)
+        fin(z - 1, 1)
+        xe1(z, 1)
+        qe1(z, 1)
+        m2(z, 1, 4)
+        fin(z, 0)
+        fin(z, 1)

import math
from contextlib import ExitStack

import concourse.mybir as mybir
from concourse.masks import make_identity

F32 = mybir.dt.float32
BF16 = mybir.dt.bfloat16
U32 = mybir.dt.uint32
U8 = mybir.dt.uint8
FP8X4 = mybir.dt.float8_e4m3fn_x4
ALU = mybir.AluOpType
ACT = mybir.ActivationFunctionType
AX = mybir.AxisListType

P = 128
NBATCH, LA, LB, D = 2, 4096, 512, 512
SCALE = 1.0 / math.sqrt(D)
NPAIR = NBATCH * LA // (2 * P)
PAIRS_PER_BATCH = NPAIR // NBATCH
NGROUP = NPAIR // 2

FLOPS = 2 * 2 * NBATCH * LA * LB * D


def tile_intra_t_kernel(tc, a, b, out):
    nc = tc.nc
    a_v = a.rearrange("n (g p t) d -> (n g) p (t d)", p=P, t=4)
    o_v = out.rearrange("n (g p t) d -> (n g) p (t d)", p=P, t=4)
    b_v = b.rearrange("n (c t) d -> n c (t d)", t=4)

    with ExitStack() as ctx:
        keep = ctx.enter_context(tc.tile_pool(name="keep", bufs=1))
        w3 = ctx.enter_context(tc.tile_pool(name="w3", bufs=3))
        w4 = ctx.enter_context(tc.tile_pool(name="w4", bufs=4))
        w6 = ctx.enter_context(tc.tile_pool(name="w6", bufs=6))
        psum = ctx.enter_context(tc.psum_pool(name="psum", bufs=1))
        ctx.enter_context(tc.manual_schedule())

        def bank(k, shape, dtype, name):
            return psum.tile(shape, dtype, tag="bank%d" % k, name=name)

        b_sb = [keep.tile([P, 4 * D], BF16, name="b_sb%d" % n) for n in range(NBATCH)]
        a_sb = [keep.tile([P, 4 * D], BF16, name="a_sb%d" % g) for g in range(NGROUP)]
        for h in range(2):
            nc.sync.dma_start(out=b_sb[0][:, h * 2 * D:(h + 1) * 2 * D], in_=b_v[0, :, h * 2 * D:(h + 1) * 2 * D])
        for h in range(2):
            nc.sync.dma_start(out=a_sb[0][:, h * 2 * D:(h + 1) * 2 * D], in_=a_v[0, :, h * 2 * D:(h + 1) * 2 * D])
        nc.sync.dma_start(out=b_sb[1][:], in_=b_v[1, :, :])
        for g in range(1, NGROUP):
            nc.sync.dma_start(out=a_sb[g][:], in_=a_v[g, :, :])

        ident_f = keep.tile([P, P], F32, name="ident_f")
        make_identity(nc, ident_f[:])
        ident_b = keep.tile([P, P], BF16, name="ident_b")
        make_identity(nc, ident_b[:])
        warm = keep.tile([P, 1], F32, name="warm")
        warm2 = keep.tile([P, 1], F32, name="warm2")
        neg1 = keep.tile([P, 2], F32, name="neg1")
        nc.vector.memset(warm[:], 0.0)
        nc.vector.memset(neg1[:], -1.0)
        nc.scalar.activation(out=warm2[:], in_=warm[:], func=ACT.Exp)

        bt_c = [keep.tile([P, LB], U32, name="bt_c%d" % n, align_bytes=64) for n in range(NBATCH)]
        bt_s = [keep.tile([P, LB], U8, name="bt_s%d" % n, align_bytes=64) for n in range(NBATCH)]
        b2_c = [keep.tile([P, D], U32, name="b2_c%d" % n, align_bytes=64) for n in range(NBATCH)]
        b2_s = [keep.tile([P, D], U8, name="b2_s%d" % n, align_bytes=64) for n in range(NBATCH)]
        gb = [keep.tile([P, 4 * D], BF16, name="gb%d" % n, align_bytes=64) for n in range(NBATCH)]

        st = {}

        def unit_src(unit, s):
            kind, x, h = unit
            src = a_sb[x] if kind == "a" else b_sb[x]
            t = 2 * h + s
            return src[:].bitcast(F32)[:, t * 256:(t + 1) * 256]

        def a_unit(j):
            return ("a", j // 2, j % 2)

        def ta(unit, k):
            at = bank(k, [P, 2, 2, P], F32, "at")
            st[("at", unit)] = at
            for s in range(2):
                src = unit_src(unit, s)
                for u in range(2):
                    nc.tensor.transpose(at[:, s, u, :], src[:, u * P:(u + 1) * P], ident_f[:])

        def xa(unit, eng):
            at = st[("at", unit)]
            ga = w4.tile([P, 8 * P], BF16, name="ga", tag="ga", align_bytes=64)
            st[("ga", unit)] = ga
            dst = ga[:].bitcast(F32).rearrange("p (s r u) -> p s r u", s=2, u=2)
            src = at[:].rearrange("p s u r -> p s r u")
            if eng == "S":
                nc.scalar.copy(out=dst, in_=src)
            else:
                nc.vector.tensor_copy(out=dst, in_=src)

        def qa(unit):
            kind, x, h = unit
            ga = st[("ga", unit)]
            if kind == "a":
                ac = w4.tile([P, 2 * P], U32, name="ac", tag="ac", align_bytes=64)
                asc = w4.tile([P, 2 * P], U8, name="asc", tag="asc", align_bytes=64)
                st[("ac", unit)] = (ac, asc)
                codes, plane = ac[:], asc[:]
            else:
                codes = bt_c[x][:, h * 256:(h + 1) * 256]
                plane = bt_s[x][:, h * 256:(h + 1) * 256]
            nc.vector.quantize_mx(out=codes.bitcast(FP8X4), scales=plane, in_=ga[:])

        def rg(n, piece, pieces, eng):
            w = D // pieces
            dst = gb[n][:, piece * 4 * w:(piece + 1) * 4 * w].rearrange("p (c i t) -> p c t i", i=4, t=4)
            src = b_sb[n][:].rearrange("p (t d) -> p t d", t=4)[:, :, piece * w:(piece + 1) * w]
            src = src.rearrange("p t (c i) -> p c t i", i=4)
            if eng == "V":
                nc.vector.tensor_copy(out=dst, in_=src)
            else:
                nc.gpsimd.tensor_scalar(out=dst, in0=src, scalar1=1.0, scalar2=0.0,
                                        op0=ALU.mult, op1=ALU.add)

        def qb2(n):
            nc.vector.quantize_mx(out=b2_c[n][:].bitcast(FP8X4), scales=b2_s[n][:], in_=gb[n][:])

        def m1(j, s):
            n = j // PAIRS_PER_BATCH
            ac, asc = st[("ac", a_unit(j))]
            sc = bank((2 * j + s) % 3, [P, LB], F32, "sc")
            st[("sc", j, s)] = sc
            nc.tensor.matmul_mx(
                out=sc[:],
                lhsT=ac[:, s * P:(s + 1) * P].bitcast(FP8X4),
                lhsT_scale=asc[:, s * P:(s + 1) * P],
                rhs=bt_c[n][:].bitcast(FP8X4),
                rhs_scale=bt_s[n][:],
                start=True,
                stop=True,
            )

        def mx_(j, s):
            if s == 0:
                st[("mx", j)] = w6.tile([P, 2], F32, name="mx", tag="mx")
                st[("nb", j)] = w6.tile([P, 2], F32, name="nb", tag="nb")
            mx = st[("mx", j)]
            nb = st[("nb", j)]
            nc.vector.reduce_max(out=mx[:, s:s + 1], in_=st[("sc", j, s)][:], axis=AX.X)
            nc.gpsimd.tensor_scalar(out=nb[:, s:s + 1], in0=mx[:, s:s + 1], scalar1=-SCALE, scalar2=0.0,
                                    op0=ALU.mult, op1=ALU.add)

        def ex(j, s):
            if s == 0:
                st[("e", j)] = w3.tile([P, 2, LB], BF16, name="e", tag="e")
                st[("rs", j)] = w6.tile([P, 2], F32, name="rs", tag="rs")
            e = st[("e", j)]
            rs = st[("rs", j)]
            nb = st[("nb", j)]
            nc.scalar.activation(out=e[:, s, :], in_=st[("sc", j, s)][:], func=ACT.Exp,
                                 bias=nb[:, s:s + 1], scale=SCALE, accum_out=rs[:, s:s + 1])

        def rc(j):
            ri = w6.tile([P, 2], F32, name="ri", tag="ri")
            st[("ri", j)] = ri
            nc.gpsimd.tensor_tensor(out=ri[:], in0=st[("rs", j)][:], in1=neg1[:], op=ALU.pow)

        def te(j):
            e = st[("e", j)]
            et = bank(6 + j % 2, [P, 2, 4, P], BF16, "et")
            st[("et", j)] = et
            for s in range(2):
                for t in range(4):
                    nc.tensor.transpose(et[:, s, t, :], e[:, s, t * P:(t + 1) * P], ident_b[:])

        def te1(j, s):
            e = st[("e", j)]
            et = bank(6 + s, [P, 4, P], BF16, "et1")
            st[("et", j, s)] = et
            for t in range(4):
                nc.tensor.transpose(et[:, t, :], e[:, s, t * P:(t + 1) * P], ident_b[:])

        def xe1(j, s):
            ge = w3.tile([P, 4 * P], BF16, name="ge1", tag="ge1", align_bytes=64)
            st[("ge", j, s)] = ge
            nc.scalar.copy(out=ge[:].rearrange("p (r t) -> p r t", t=4),
                           in_=st[("et", j, s)][:].rearrange("p t r -> p r t"))

        def qe1(j, s):
            if s == 0:
                ec = w3.tile([P, 2 * P], U32, name="ec", tag="ec", align_bytes=64)
                es = w3.tile([P, 2 * P], U8, name="es", tag="es", align_bytes=64)
                st[("ec", j)] = (ec, es)
            ec, es = st[("ec", j)]
            nc.vector.quantize_mx(out=ec[:, s * P:(s + 1) * P].bitcast(FP8X4), scales=es[:, s * P:(s + 1) * P],
                                  in_=st[("ge", j, s)][:])

        def xe(j):
            et = st[("et", j)]
            ge = w3.tile([P, 8 * P], BF16, name="ge", tag="ge", align_bytes=64)
            st[("ge", j)] = ge
            nc.scalar.copy(out=ge[:].rearrange("p (s r t) -> p s r t", s=2, t=4),
                           in_=et[:].rearrange("p s t r -> p s r t"))

        def qe(j):
            ec = w3.tile([P, 2 * P], U32, name="ec", tag="ec", align_bytes=64)
            es = w3.tile([P, 2 * P], U8, name="es", tag="es", align_bytes=64)
            st[("ec", j)] = (ec, es)
            nc.vector.quantize_mx(out=ec[:].bitcast(FP8X4), scales=es[:], in_=st[("ge", j)][:])

        def m2(j, s, k):
            n = j // PAIRS_PER_BATCH
            ec, es = st[("ec", j)]
            oc = bank(k, [P, D], F32, "oc")
            st[("oc", j, s)] = oc
            nc.tensor.matmul_mx(
                out=oc[:],
                lhsT=ec[:, s * P:(s + 1) * P].bitcast(FP8X4),
                lhsT_scale=es[:, s * P:(s + 1) * P],
                rhs=b2_c[n][:].bitcast(FP8X4),
                rhs_scale=b2_s[n][:],
                start=True,
                stop=True,
            )

        def fin(j, s):
            g, h = j // 2, j % 2
            if s == 0:
                st[("ob", j)] = w4.tile([P, 2, D], F32, name="ob", tag="ob")
            ob = st[("ob", j)]
            ri = st[("ri", j)]
            t = 2 * h + s
            nc.vector.scalar_tensor_tensor(
                out=ob[:, s, :], in0=st[("oc", j, s)][:], scalar=ri[:, s:s + 1],
                in1=a_sb[g][:, t * D:(t + 1) * D], op0=ALU.mult, op1=ALU.add)
            if j == NPAIR - 1:
                nc.sync.dma_start(out=o_v[g, :, t * D:(t + 1) * D], in_=ob[:, s, :])
            elif s == 1:
                nc.sync.dma_start(out=o_v[g, :, h * 2 * D:(h + 1) * 2 * D],
                                  in_=ob[:].rearrange("p s d -> p (s d)"))

        ub = [[("b", n, h) for h in range(2)] for n in range(NBATCH)]
        ta(ub[0][0], 5)
        ta(ub[0][1], 6)
        xa(ub[0][0], "S")
        rg(0, 0, 2, "V")
        xa(ub[0][1], "V")
        ta(a_unit(0), 7)
        ta(a_unit(1), 3)
        qa(ub[0][0])
        qa(ub[0][1])
        xa(a_unit(0), "S")
        xa(a_unit(1), "S")
        qa(a_unit(0))
        qa(a_unit(1))
        rg(0, 1, 2, "V")
        ta(ub[1][0], 4)
        ta(ub[1][1], 2)
        m1(0, 0)
        m1(0, 1)
        xa(ub[1][0], "S")
        xa(ub[1][1], "S")
        m1(1, 0)
        ta(a_unit(2), 5)
        mx_(0, 0)
        mx_(0, 1)
        qb2(0)

        def live(j):
            return 0 <= j < NPAIR

        for i in range(0, NPAIR - 1):
            if i == 3:
                qb2(1)
            if live(i - 2):
                qe(i - 2)
                m2(i - 2, 0, 3)
            if live(i + 1):
                mx_(i + 1, 0)
            if i == 0:
                qa(ub[1][0])
                qa(ub[1][1])
            if i <= 1:
                rg(1, 2 * i, 4, "G")
            if 3 <= i + 2 < NPAIR:
                qa(a_unit(i + 2))
            if live(i):
                ex(i, 0)
            if live(i + 1):
                m1(i + 1, 1)
            if live(i):
                ex(i, 1)
                rc(i)
            if i == 0:
                xa(a_unit(2), "S")
                qa(a_unit(2))
            if 3 <= i + 3 < NPAIR:
                ta(a_unit(i + 3), 5)
            if live(i):
                te(i)
            if live(i - 3):
                fin(i - 3, 1)
            if live(i - 2):
                m2(i - 2, 1, 4)
            if live(i + 2):
                m1(i + 2, 0)
            if live(i - 1):
                xe(i - 1)
            if 3 <= i + 3 < NPAIR:
                xa(a_unit(i + 3), "S")
            if live(i + 1):
                mx_(i + 1, 1)
            if i <= 1:
                rg(1, 2 * i + 1, 4, "G")
            if live(i - 2):
                fin(i - 2, 0)

        z = NPAIR - 1
        qe(z - 2)
        m2(z - 2, 0, 3)
        fin(z - 3, 1)
        m2(z - 2, 1, 4)
        xe(z - 1)
        qe(z - 1)
        ex(z, 0)
        te1(z, 0)
        m2(z - 1, 0, 1)
        m2(z - 1, 1, 5)
        ex(z, 1)
        rc(z)
        te1(z, 1)
        fin(z - 2, 0)
        fin(z - 2, 1)
        fin(z - 1, 0)
        xe1(z, 0)
        qe1(z, 0)
        m2(z, 0, 3)
        fin(z - 1, 1)
        xe1(z, 1)
        qe1(z, 1)
        m2(z, 1, 4)
        fin(z, 0)
        fin(z, 1)
